import numpy as np
import ml_dtypes


def mxq(x, axis, fmt="e4m3"):
    dtype, down = {"e4m3": (ml_dtypes.float8_e4m3fn, 7), "e5m2": (ml_dtypes.float8_e5m2, 14)}[fmt]
    v = np.moveaxis(np.asarray(x, np.float32).astype(ml_dtypes.bfloat16).astype(np.float64), axis, -1)
    blocks = v.reshape(v.shape[:-1] + (-1, 32))
    amax = np.abs(blocks).max(-1, keepdims=True)
    byte = np.maximum(np.where(amax > 0, np.frexp(amax)[1] - 1 + 127, 0) - down, 1)
    scale = np.exp2(byte - 127.0)
    codes = (blocks / scale).astype(np.float32).astype(dtype).astype(np.float64)
    return np.moveaxis((codes * scale).reshape(v.shape), -1, axis)


WIDE = False


def mx_kscale(k):
    if not WIDE:
        return np.ones(k)
    levels = np.array([10, -10, 5, -5, 0])
    a = np.random.permutation(np.resize(levels, k // 512 * 4)).reshape(k // 512, 4)
    idx = np.arange(k)
    return np.exp2(a[idx // 512, idx % 128 // 32])


BF16 = ml_dtypes.bfloat16


def bf(x):
    return np.asarray(x, np.float32).astype(BF16)


def f64(x):
    return np.asarray(x).astype(np.float64)


B, S, D, H, HKV, HD, WINDOW, KB = 1, 512, 2048, 16, 8, 128, 256, 512
EPS = 1e-6
THETA = 10000.0


def rope_tables():
    inv_freq = 1.0 / THETA ** (np.arange(0, HD, 2) / HD)
    ang = np.arange(S)[:, None] * inv_freq[None, :]
    emb = np.concatenate([ang, ang], axis=-1)
    return np.broadcast_to(np.cos(emb)[None], (B, S, HD)), np.broadcast_to(np.sin(emb)[None], (B, S, HD))


def rms_norm(x, gain):
    var = np.mean(x * x, axis=-1, keepdims=True)
    return x * (1.0 / np.sqrt(var + EPS)) * gain


def rotate_half(x):
    return np.concatenate([-x[..., HD // 2:], x[..., :HD // 2]], axis=-1)


def apply_rope(x, cos, sin):
    return x * cos[:, :, None, :] + rotate_half(x) * sin[:, :, None, :]


def setup_inputs():
    s = mx_kscale(D)
    cos, sin = rope_tables()
    return {
        "hidden_states": bf(np.random.standard_normal((B, S, D)) * s),
        "cos": bf(cos),
        "sin": bf(sin),
        "Wq": bf(np.random.standard_normal((D, H * HD)) / np.sqrt(D) / s[:, None]),
        "Wk": bf(np.random.standard_normal((D, HKV * HD)) / np.sqrt(D) / s[:, None]),
        "Wv": bf(np.random.standard_normal((D, HKV * HD)) * 2.0 / np.sqrt(D) / s[:, None]),
        "q_scale": bf(np.random.uniform(0.5, 1.5, HD)),
        "k_scale": bf(np.random.uniform(0.5, 1.5, HD)),
    }


def reference(hidden_states, cos, sin, Wq, Wk, Wv, q_scale, k_scale):
    xq = mxq(f64(hidden_states), 2, "e4m3")
    q = (xq @ mxq(f64(Wq), 0, "e4m3")).reshape(B, S, H, HD)
    k = (xq @ mxq(f64(Wk), 0, "e4m3")).reshape(B, S, HKV, HD)
    v = (xq @ mxq(f64(Wv), 0, "e4m3")).reshape(B, S, HKV, HD)
    q = rms_norm(q, f64(q_scale))
    k = rms_norm(k, f64(k_scale))
    q = apply_rope(q, f64(cos), f64(sin))
    k = apply_rope(k, f64(cos), f64(sin))
    return q, k, v

@@ -1,0 +1,269 @@
+from contextlib import ExitStack
+
+import concourse.mybir as mybir
+from concourse.masks import make_identity
+
+F32 = mybir.dt.float32
+BF16 = mybir.dt.bfloat16
+U32 = mybir.dt.uint32
+U8 = mybir.dt.uint8
+FP8X4 = mybir.dt.float8_e4m3fn_x4
+ACT = mybir.ActivationFunctionType
+ALU = mybir.AluOpType
+
+P = 128
+PACK = 4
+K_PASS = P * PACK
+POSITIONS = 512
+MODEL_DIM = 2048
+HEAD_DIM = 128
+HALF = HEAD_DIM // 2
+EPS = 1e-6
+
+PASSES = MODEL_DIM // K_PASS
+POSITION_TILES = POSITIONS // P
+UNIT_COLS = 512
+UNIT_HEADS = UNIT_COLS // HEAD_DIM
+
+VECTOR_COLS = 208
+RUN = 4
+
+UNITS_LOADED_AHEAD = 3
+
+FLOPS = 2 * POSITIONS * MODEL_DIM * (2048 + 1024 + 1024)
+
+
+def tile_multiheadattention_pa_kernel(
+    tc, hidden_states, cos, sin, Wq, Wk, Wv, q_scale, k_scale, out_0, out_1, out_2
+):
+    nc = tc.nc
+    x_rows = hidden_states.rearrange("b s k -> (b s) k")
+    q_rows = out_0.rearrange("b s h d -> (b s) (h d)")
+    k_rows = out_1.rearrange("b s h d -> (b s) (h d)")
+    v_rows = out_2.rearrange("b s h d -> (b s) (h d)")
+
+    with ExitStack() as ctx:
+        const = ctx.enter_context(tc.tile_pool(name="const", bufs=1))
+        x_stage = ctx.enter_context(tc.tile_pool(name="x_stage", bufs=2))
+        raw_pool = ctx.enter_context(tc.tile_pool(name="raw", bufs=UNITS_LOADED_AHEAD * PASSES))
+        grouped_pool = ctx.enter_context(tc.tile_pool(name="grouped", bufs=3))
+        packed_pool = ctx.enter_context(tc.tile_pool(name="packed", bufs=2 * PASSES))
+        result_pool = ctx.enter_context(tc.tile_pool(name="result", bufs=3))
+        scratch_pool = ctx.enter_context(tc.tile_pool(name="scratch", bufs=2))
+        psum = ctx.enter_context(tc.psum_pool(name="psum", bufs=8))
+
+        units = []
+        for weight, rows, tables_name in ((Wq, q_rows, "q"), (Wk, k_rows, "k"), (Wv, v_rows, None)):
+            for first_col in range(0, weight.shape[1], UNIT_COLS):
+                units.append((weight, rows, tables_name, first_col))
+
+        raw_chunks = {}
+
+        def load_weight_chunk(n, g):
+            weight, first_col = units[n][0], units[n][3]
+            raw = raw_pool.tile([P, PACK, UNIT_COLS], BF16, name="raw")
+            nc.sync.dma_start(
+                out=raw[:],
+                in_=weight[g * K_PASS : (g + 1) * K_PASS, first_col : first_col + UNIT_COLS].rearrange(
+                    "(p t) c -> p t c", t=PACK
+                ),
+            )
+            raw_chunks[(n, g)] = raw
+
+        x_tiles = []
+        for m in range(POSITION_TILES):
+            load_weight_chunk(0, m)
+            x_tile = const.tile([P, MODEL_DIM], BF16, name="x_tile%d" % m)
+            nc.sync.dma_start(out=x_tile[:], in_=x_rows[m * P : (m + 1) * P, :])
+            x_tiles.append(x_tile)
+        for n in range(1, UNITS_LOADED_AHEAD):
+            for g in range(PASSES):
+                load_weight_chunk(n, g)
+
+        cos_sb = const.tile([P, POSITION_TILES, HEAD_DIM], BF16)
+        nc.sync.dma_start(out=cos_sb[:], in_=cos.rearrange("b s d -> (b s) d").rearrange("(m p) d -> p m d", p=P))
+        sin_sb = const.tile([P, POSITION_TILES, HEAD_DIM], BF16)
+        nc.sync.dma_start(out=sin_sb[:], in_=sin.rearrange("b s d -> (b s) d").rearrange("(m p) d -> p m d", p=P))
+        gains = {}
+        for tables_name, gain in (("q", q_scale), ("k", k_scale)):
+            gain_sb = const.tile([P, HEAD_DIM], BF16, name="gain_" + tables_name)
+            nc.sync.dma_start(out=gain_sb[:], in_=gain.partition_broadcast(P))
+            gains[tables_name] = gain_sb
+
+        identity = const.tile([P, P], F32)
+        make_identity(nc, identity[:])
+        eps_column = const.tile([P, 1], F32)
+        nc.vector.memset(eps_column[:], EPS)
+
+        x_words = const.tile([P, PASSES, POSITIONS], U32, align_bytes=64)
+        x_scales = const.tile([P, PASSES, POSITIONS], U8, align_bytes=64)
+        pairs = PACK // 2
+        for g in range(PASSES):
+            x_grouped = x_stage.tile([P, POSITIONS, PACK], BF16, align_bytes=64)
+            x_grouped_f32 = x_grouped[:].bitcast(F32)
+            for first_tile in range(0, POSITION_TILES, 2):
+                turned = psum.tile([P, pairs, 2 * P], F32, name="turned", tag="bank")
+                for i in range(2):
+                    words = x_tiles[first_tile + i][:].bitcast(F32).rearrange(
+                        "s (g p u) -> s g u p", g=PASSES, u=pairs
+                    )
+                    for u in range(pairs):
+                        nc.tensor.transpose(turned[:, u, i * P : (i + 1) * P], words[:, g, u, :], identity[:])
+                nc.scalar.copy(
+                    out=x_grouped_f32[:, first_tile * P : (first_tile + 2) * P, :],
+                    in_=turned[:].rearrange("p u s -> p s u"),
+                )
+            nc.vector.quantize_mx(
+                out=x_words[:, g, :].bitcast(FP8X4),
+                scales=x_scales[:, g, :],
+                in_=x_grouped[:].rearrange("p s t -> p (s t)"),
+            )
+
+        low, high = slice(0, HALF), slice(HALF, HEAD_DIM)
+        tables = {}
+        for tables_name in ("q", "k"):
+            gain_sb = gains[tables_name]
+            straight = const.tile([P, POSITION_TILES, HEAD_DIM], F32, name="straight_" + tables_name)
+            crossed = const.tile([P, POSITION_TILES, HEAD_DIM], F32, name="crossed_" + tables_name)
+            nc.vector.tensor_tensor(
+                out=straight[:],
+                in0=cos_sb[:],
+                in1=gain_sb[:].unsqueeze(1).to_broadcast([P, POSITION_TILES, HEAD_DIM]),
+                op=ALU.mult,
+            )
+            nc.vector.scalar_tensor_tensor(
+                out=crossed[:, :, low],
+                in0=sin_sb[:, :, low],
+                scalar=-1.0,
+                in1=gain_sb[:, high].unsqueeze(1).to_broadcast([P, POSITION_TILES, HALF]),
+                op0=ALU.mult,
+                op1=ALU.mult,
+            )
+            nc.vector.tensor_tensor(
+                out=crossed[:, :, high],
+                in0=sin_sb[:, :, high],
+                in1=gain_sb[:, low].unsqueeze(1).to_broadcast([P, POSITION_TILES, HALF]),
+                op=ALU.mult,
+            )
+            tables[tables_name] = (straight, crossed)
+
+        def regroup(n, g):
+            raw = raw_chunks[(n, g)]
+            grouped = grouped_pool.tile([P, UNIT_COLS, PACK], BF16, align_bytes=64, name="grouped")
+            nc.vector.tensor_copy(
+                out=grouped[:, :VECTOR_COLS, :].rearrange("p (c i) t -> p c t i", i=RUN),
+                in_=raw[:, :, :VECTOR_COLS].rearrange("p t (c i) -> p c t i", i=RUN),
+            )
+            nc.scalar.copy(
+                out=grouped[:, VECTOR_COLS:, :].rearrange("p (c i) t -> p c t i", i=RUN),
+                in_=raw[:, :, VECTOR_COLS:].rearrange("p t (c i) -> p c t i", i=RUN),
+            )
+            return grouped
+
+        def quantise_and_multiply(grouped, g, banks):
+            w_words = packed_pool.tile([P, UNIT_COLS], U32, align_bytes=64, name="w_words")
+            w_scales = packed_pool.tile([P, UNIT_COLS], U8, align_bytes=64, name="w_scales")
+            nc.vector.quantize_mx(
+                out=w_words[:].bitcast(FP8X4),
+                scales=w_scales[:],
+                in_=grouped[:].rearrange("p c t -> p (c t)"),
+            )
+            for m in range(POSITION_TILES):
+                positions = slice(m * P, (m + 1) * P)
+                nc.tensor.matmul_mx(
+                    out=banks[m][:],
+                    lhsT=x_words[:, g, positions].bitcast(FP8X4),
+                    lhsT_scale=x_scales[:, g, positions],
+                    rhs=w_words[:].bitcast(FP8X4),
+                    rhs_scale=w_scales[:],
+                    start=(g == 0),
+                    stop=(g == PASSES - 1),
+                )
+
+        def multiply_unit(n):
+            banks = [psum.tile([P, UNIT_COLS], F32, name="bank", tag="bank") for m in range(POSITION_TILES)]
+            waiting = regroup(n, 0)
+            for g in range(1, PASSES):
+                grouped = regroup(n, g)
+                quantise_and_multiply(waiting, g - 1, banks)
+                waiting = grouped
+            quantise_and_multiply(waiting, PASSES - 1, banks)
+            return banks
+
+        def store(n, m, result):
+            rows, first_col = units[n][1], units[n][3]
+            nc.sync.dma_start(
+                out=rows[m * P : (m + 1) * P, first_col : first_col + UNIT_COLS], in_=result[:, m, :]
+            )
+
+        def finish_plain(n, banks):
+            result = result_pool.tile([P, POSITION_TILES, UNIT_COLS], F32, name="result")
+            for m in range(POSITION_TILES):
+                copy = nc.scalar.copy if m % 2 == 0 else nc.vector.tensor_copy
+                copy(out=result[:, m, :], in_=banks[m][:])
+                store(n, m, result)
+
+        def finish_normed_and_rotated(n, banks):
+            straight, crossed = tables[units[n][2]]
+            result = result_pool.tile([P, POSITION_TILES, UNIT_COLS], F32, name="result")
+            cross_term = scratch_pool.tile([P, POSITION_TILES, UNIT_COLS], F32, name="cross_term")
+            squares = scratch_pool.tile([P, POSITION_TILES, UNIT_COLS], BF16, name="squares")
+            square_sums = scratch_pool.tile([P, POSITION_TILES * UNIT_HEADS], F32, name="square_sums")
+            rms = scratch_pool.tile([P, POSITION_TILES * UNIT_HEADS], F32, name="rms")
+            rinv = scratch_pool.tile([P, POSITION_TILES * UNIT_HEADS], F32, name="rinv")
+
+            for m in range(POSITION_TILES):
+                for h in range(UNIT_HEADS):
+                    head = slice(h * HEAD_DIM, (h + 1) * HEAD_DIM)
+                    column = m * UNIT_HEADS + h
+                    nc.scalar.activation(
+                        out=squares[:, m, head],
+                        in_=banks[m][:, head],
+                        func=ACT.Square,
+                        accum_out=square_sums[:, column : column + 1],
+                    )
+                u = banks[m][:].rearrange("p (h d) -> p h d", d=HEAD_DIM)
+                nc.vector.tensor_tensor(
+                    out=result[:, m, :].rearrange("p (h d) -> p h d", d=HEAD_DIM),
+                    in0=u,
+                    in1=straight[:, m, :].unsqueeze(1).to_broadcast([P, UNIT_HEADS, HEAD_DIM]),
+                    op=ALU.mult,
+                )
+                cross = cross_term[:, m, :].rearrange("p (h d) -> p h d", d=HEAD_DIM)
+                for here, there in ((low, high), (high, low)):
+                    nc.vector.tensor_tensor(
+                        out=cross[:, :, here],
+                        in0=u[:, :, there],
+                        in1=crossed[:, m, here].unsqueeze(1).to_broadcast([P, UNIT_HEADS, HALF]),
+                        op=ALU.mult,
+                    )
+
+            nc.scalar.activation(
+                out=rms[:], in_=square_sums[:], func=ACT.Sqrt, scale=1.0 / HEAD_DIM, bias=eps_column[:]
+            )
+            nc.vector.reciprocal(out=rinv[:], in_=rms[:])
+            nc.vector.tensor_tensor(out=result[:], in0=result[:], in1=cross_term[:], op=ALU.add)
+
+            for m in range(POSITION_TILES):
+                for h in range(UNIT_HEADS):
+                    head = slice(h * HEAD_DIM, (h + 1) * HEAD_DIM)
+                    column = m * UNIT_HEADS + h
+                    nc.scalar.activation(
+                        out=result[:, m, head],
+                        in_=result[:, m, head],
+                        func=ACT.Copy,
+                        scale=rinv[:, column : column + 1],
+                    )
+                store(n, m, result)
+
+        banks_of = {0: multiply_unit(0)}
+        for n in range(len(units)):
+            if n + UNITS_LOADED_AHEAD < len(units):
+                for g in range(PASSES):
+                    load_weight_chunk(n + UNITS_LOADED_AHEAD, g)
+            if n + 1 < len(units):
+                banks_of[n + 1] = multiply_unit(n + 1)
+            if units[n][2] is None:
+                finish_plain(n, banks_of[n])
+            else:
+                finish_normed_and_rotated(n, banks_of[n])

@@ -13,6 +13,7 @@ ALU = mybir.AluOpType
 
 P = 128
 PACK = 4
+PAIRS = PACK // 2
 K_PASS = P * PACK
 POSITIONS = 512
 MODEL_DIM = 2048
@@ -21,14 +22,19 @@ HALF = HEAD_DIM // 2
 EPS = 1e-6
 
 PASSES = MODEL_DIM // K_PASS
-POSITION_TILES = POSITIONS // P
+TILES = POSITIONS // P
 UNIT_COLS = 512
 UNIT_HEADS = UNIT_COLS // HEAD_DIM
 
 VECTOR_COLS = 208
 RUN = 4
 
-UNITS_LOADED_AHEAD = 3
+REGROUP_AHEAD = PASSES
+SQUARES_AFTER = PASSES
+PRODUCTS_AFTER = SQUARES_AFTER + 1
+INVERT_AFTER = SQUARES_AFTER + TILES
+SCALE_AFTER = INVERT_AFTER + 1
+RAW_CHUNKS = 12
 
 FLOPS = 2 * POSITIONS * MODEL_DIM * (2048 + 1024 + 1024)
 
@@ -41,25 +47,36 @@ def tile_multiheadattention_pa_kernel(
     q_rows = out_0.rearrange("b s h d -> (b s) (h d)")
     k_rows = out_1.rearrange("b s h d -> (b s) (h d)")
     v_rows = out_2.rearrange("b s h d -> (b s) (h d)")
+    low, high = slice(0, HALF), slice(HALF, HEAD_DIM)
+
+    units = []
+    for weight, rows, tables_name in ((Wq, q_rows, "q"), (Wk, k_rows, "k"), (Wv, v_rows, None)):
+        for first_col in range(0, weight.shape[1], UNIT_COLS):
+            units.append((weight, rows, tables_name, first_col))
+    chunks = len(units) * PASSES
+    banks = len(units) * TILES
 
     with ExitStack() as ctx:
+        ctx.enter_context(tc.manual_schedule())
         const = ctx.enter_context(tc.tile_pool(name="const", bufs=1))
         x_stage = ctx.enter_context(tc.tile_pool(name="x_stage", bufs=2))
-        raw_pool = ctx.enter_context(tc.tile_pool(name="raw", bufs=UNITS_LOADED_AHEAD * PASSES))
-        grouped_pool = ctx.enter_context(tc.tile_pool(name="grouped", bufs=3))
+        raw_pool = ctx.enter_context(tc.tile_pool(name="raw", bufs=RAW_CHUNKS))
+        grouped_pool = ctx.enter_context(tc.tile_pool(name="grouped", bufs=REGROUP_AHEAD + 2))
         packed_pool = ctx.enter_context(tc.tile_pool(name="packed", bufs=2 * PASSES))
-        result_pool = ctx.enter_context(tc.tile_pool(name="result", bufs=3))
-        scratch_pool = ctx.enter_context(tc.tile_pool(name="scratch", bufs=2))
+        result_pool = ctx.enter_context(tc.tile_pool(name="result", bufs=SCALE_AFTER - PRODUCTS_AFTER + 4))
+        scratch_pool = ctx.enter_context(tc.tile_pool(name="scratch", bufs=3))
         psum = ctx.enter_context(tc.psum_pool(name="psum", bufs=8))
 
-        units = []
-        for weight, rows, tables_name in ((Wq, q_rows, "q"), (Wk, k_rows, "k"), (Wv, v_rows, None)):
-            for first_col in range(0, weight.shape[1], UNIT_COLS):
-                units.append((weight, rows, tables_name, first_col))
+        raw_of = {}
+        grouped_of = {}
+        bank_of = {}
+        result_of = {}
+        cross_of = {}
+        norm_of = {}
+        tables = {}
 
-        raw_chunks = {}
-
-        def load_weight_chunk(n, g):
+        def load_chunk(j):
+            n, g = divmod(j, PASSES)
             weight, first_col = units[n][0], units[n][3]
             raw = raw_pool.tile([P, PACK, UNIT_COLS], BF16, name="raw")
             nc.sync.dma_start(
@@ -68,87 +85,10 @@ def tile_multiheadattention_pa_kernel(
                     "(p t) c -> p t c", t=PACK
                 ),
             )
-            raw_chunks[(n, g)] = raw
+            raw_of[j] = raw
 
-        x_tiles = []
-        for m in range(POSITION_TILES):
-            load_weight_chunk(0, m)
-            x_tile = const.tile([P, MODEL_DIM], BF16, name="x_tile%d" % m)
-            nc.sync.dma_start(out=x_tile[:], in_=x_rows[m * P : (m + 1) * P, :])
-            x_tiles.append(x_tile)
-        for n in range(1, UNITS_LOADED_AHEAD):
-            for g in range(PASSES):
-                load_weight_chunk(n, g)
-
-        cos_sb = const.tile([P, POSITION_TILES, HEAD_DIM], BF16)
-        nc.sync.dma_start(out=cos_sb[:], in_=cos.rearrange("b s d -> (b s) d").rearrange("(m p) d -> p m d", p=P))
-        sin_sb = const.tile([P, POSITION_TILES, HEAD_DIM], BF16)
-        nc.sync.dma_start(out=sin_sb[:], in_=sin.rearrange("b s d -> (b s) d").rearrange("(m p) d -> p m d", p=P))
-        gains = {}
-        for tables_name, gain in (("q", q_scale), ("k", k_scale)):
-            gain_sb = const.tile([P, HEAD_DIM], BF16, name="gain_" + tables_name)
-            nc.sync.dma_start(out=gain_sb[:], in_=gain.partition_broadcast(P))
-            gains[tables_name] = gain_sb
-
-        identity = const.tile([P, P], F32)
-        make_identity(nc, identity[:])
-        eps_column = const.tile([P, 1], F32)
-        nc.vector.memset(eps_column[:], EPS)
-
-        x_words = const.tile([P, PASSES, POSITIONS], U32, align_bytes=64)
-        x_scales = const.tile([P, PASSES, POSITIONS], U8, align_bytes=64)
-        pairs = PACK // 2
-        for g in range(PASSES):
-            x_grouped = x_stage.tile([P, POSITIONS, PACK], BF16, align_bytes=64)
-            x_grouped_f32 = x_grouped[:].bitcast(F32)
-            for first_tile in range(0, POSITION_TILES, 2):
-                turned = psum.tile([P, pairs, 2 * P], F32, name="turned", tag="bank")
-                for i in range(2):
-                    words = x_tiles[first_tile + i][:].bitcast(F32).rearrange(
-                        "s (g p u) -> s g u p", g=PASSES, u=pairs
-                    )
-                    for u in range(pairs):
-                        nc.tensor.transpose(turned[:, u, i * P : (i + 1) * P], words[:, g, u, :], identity[:])
-                nc.scalar.copy(
-                    out=x_grouped_f32[:, first_tile * P : (first_tile + 2) * P, :],
-                    in_=turned[:].rearrange("p u s -> p s u"),
-                )
-            nc.vector.quantize_mx(
-                out=x_words[:, g, :].bitcast(FP8X4),
-                scales=x_scales[:, g, :],
-                in_=x_grouped[:].rearrange("p s t -> p (s t)"),
-            )
-
-        low, high = slice(0, HALF), slice(HALF, HEAD_DIM)
-        tables = {}
-        for tables_name in ("q", "k"):
-            gain_sb = gains[tables_name]
-            straight = const.tile([P, POSITION_TILES, HEAD_DIM], F32, name="straight_" + tables_name)
-            crossed = const.tile([P, POSITION_TILES, HEAD_DIM], F32, name="crossed_" + tables_name)
-            nc.vector.tensor_tensor(
-                out=straight[:],
-                in0=cos_sb[:],
-                in1=gain_sb[:].unsqueeze(1).to_broadcast([P, POSITION_TILES, HEAD_DIM]),
-                op=ALU.mult,
-            )
-            nc.vector.scalar_tensor_tensor(
-                out=crossed[:, :, low],
-                in0=sin_sb[:, :, low],
-                scalar=-1.0,
-                in1=gain_sb[:, high].unsqueeze(1).to_broadcast([P, POSITION_TILES, HALF]),
-                op0=ALU.mult,
-                op1=ALU.mult,
-            )
-            nc.vector.tensor_tensor(
-                out=crossed[:, :, high],
-                in0=sin_sb[:, :, high],
-                in1=gain_sb[:, low].unsqueeze(1).to_broadcast([P, POSITION_TILES, HALF]),
-                op=ALU.mult,
-            )
-            tables[tables_name] = (straight, crossed)
-
-        def regroup(n, g):
-            raw = raw_chunks[(n, g)]
+        def regroup(j):
+            raw = raw_of[j]
             grouped = grouped_pool.tile([P, UNIT_COLS, PACK], BF16, align_bytes=64, name="grouped")
             nc.vector.tensor_copy(
                 out=grouped[:, :VECTOR_COLS, :].rearrange("p (c i) t -> p c t i", i=RUN),
@@ -158,112 +98,212 @@ def tile_multiheadattention_pa_kernel(
                 out=grouped[:, VECTOR_COLS:, :].rearrange("p (c i) t -> p c t i", i=RUN),
                 in_=raw[:, :, VECTOR_COLS:].rearrange("p t (c i) -> p c t i", i=RUN),
             )
-            return grouped
+            grouped_of[j] = grouped
+            if j + RAW_CHUNKS < chunks:
+                load_chunk(j + RAW_CHUNKS)
 
-        def quantise_and_multiply(grouped, g, banks):
+        def quantise_and_multiply(j):
+            n, g = divmod(j, PASSES)
             w_words = packed_pool.tile([P, UNIT_COLS], U32, align_bytes=64, name="w_words")
             w_scales = packed_pool.tile([P, UNIT_COLS], U8, align_bytes=64, name="w_scales")
             nc.vector.quantize_mx(
                 out=w_words[:].bitcast(FP8X4),
                 scales=w_scales[:],
-                in_=grouped[:].rearrange("p c t -> p (c t)"),
+                in_=grouped_of[j][:].rearrange("p c t -> p (c t)"),
             )
-            for m in range(POSITION_TILES):
-                positions = slice(m * P, (m + 1) * P)
+            for m in range(TILES):
+                b = n * TILES + m
+                if g == 0:
+                    bank_of[b] = psum.tile([P, UNIT_COLS], F32, name="bank", tag="bank")
                 nc.tensor.matmul_mx(
-                    out=banks[m][:],
-                    lhsT=x_words[:, g, positions].bitcast(FP8X4),
-                    lhsT_scale=x_scales[:, g, positions],
+                    out=bank_of[b][:],
+                    lhsT=x_words[:, m, g, :].bitcast(FP8X4),
+                    lhsT_scale=x_scales[:, m, g, :],
                     rhs=w_words[:].bitcast(FP8X4),
                     rhs_scale=w_scales[:],
                     start=(g == 0),
                     stop=(g == PASSES - 1),
                 )
 
-        def multiply_unit(n):
-            banks = [psum.tile([P, UNIT_COLS], F32, name="bank", tag="bank") for m in range(POSITION_TILES)]
-            waiting = regroup(n, 0)
-            for g in range(1, PASSES):
-                grouped = regroup(n, g)
-                quantise_and_multiply(waiting, g - 1, banks)
-                waiting = grouped
-            quantise_and_multiply(waiting, PASSES - 1, banks)
-            return banks
+        def turn_and_quantise_positions(m):
+            x_grouped = x_stage.tile([P, PASSES, P, PACK], BF16, align_bytes=64, name="x_grouped")
+            x_grouped_f32 = x_grouped[:].bitcast(F32)
+            words = x_tiles[m][:].bitcast(F32).rearrange("s (g p u) -> s g u p", g=PASSES, u=PAIRS)
+            for first_pass, copy in ((0, nc.scalar.copy), (2, nc.vector.tensor_copy)):
+                turned = psum.tile([P, 2, PAIRS, P], F32, name="turned", tag="bank")
+                for i in range(2):
+                    for u in range(PAIRS):
+                        nc.tensor.transpose(turned[:, i, u, :], words[:, first_pass + i, u, :], identity[:])
+                copy(
+                    out=x_grouped_f32[:, first_pass : first_pass + 2, :, :],
+                    in_=turned[:].rearrange("p g u s -> p g s u"),
+                )
+            nc.vector.quantize_mx(
+                out=x_words[:, m, :, :].rearrange("p g s -> p (g s)").bitcast(FP8X4),
+                scales=x_scales[:, m, :, :].rearrange("p g s -> p (g s)"),
+                in_=x_grouped[:].rearrange("p g s t -> p (g s t)"),
+            )
 
-        def store(n, m, result):
+        def build_tables(tables_name, gain_sb):
+            straight = const.tile([P, TILES, HEAD_DIM], F32, name="straight_" + tables_name)
+            crossed = const.tile([P, TILES, HEAD_DIM], F32, name="crossed_" + tables_name)
+            nc.vector.tensor_tensor(
+                out=straight[:],
+                in0=cos_sb[:],
+                in1=gain_sb[:].unsqueeze(1).to_broadcast([P, TILES, HEAD_DIM]),
+                op=ALU.mult,
+            )
+            nc.vector.scalar_tensor_tensor(
+                out=crossed[:, :, low],
+                in0=sin_sb[:, :, low],
+                scalar=-1.0,
+                in1=gain_sb[:, high].unsqueeze(1).to_broadcast([P, TILES, HALF]),
+                op0=ALU.mult,
+                op1=ALU.mult,
+            )
+            nc.vector.tensor_tensor(
+                out=crossed[:, :, high],
+                in0=sin_sb[:, :, high],
+                in1=gain_sb[:, low].unsqueeze(1).to_broadcast([P, TILES, HALF]),
+                op=ALU.mult,
+            )
+            tables[tables_name] = (straight, crossed)
+
+        def store(b):
+            n, m = divmod(b, TILES)
             rows, first_col = units[n][1], units[n][3]
             nc.sync.dma_start(
-                out=rows[m * P : (m + 1) * P, first_col : first_col + UNIT_COLS], in_=result[:, m, :]
+                out=rows[m * P : (m + 1) * P, first_col : first_col + UNIT_COLS],
+                in_=result_of[b][:].rearrange("p h d -> p (h d)"),
             )
 
-        def finish_plain(n, banks):
-            result = result_pool.tile([P, POSITION_TILES, UNIT_COLS], F32, name="result")
-            for m in range(POSITION_TILES):
-                copy = nc.scalar.copy if m % 2 == 0 else nc.vector.tensor_copy
-                copy(out=result[:, m, :], in_=banks[m][:])
-                store(n, m, result)
+        def sum_squares(b):
+            n, m = divmod(b, TILES)
+            if m == 0:
+                norm_of[n] = [
+                    scratch_pool.tile([P, TILES * UNIT_HEADS], F32, name=name)
+                    for name in ("square_sums", "rms", "rinv")
+                ]
+            square_sums, rms = norm_of[n][0], norm_of[n][1]
+            squares = scratch_pool.tile([P, UNIT_COLS], BF16, name="squares")
+            for h in range(UNIT_HEADS):
+                head = slice(h * HEAD_DIM, (h + 1) * HEAD_DIM)
+                column = m * UNIT_HEADS + h
+                nc.scalar.activation(
+                    out=squares[:, head],
+                    in_=bank_of[b][:, head],
+                    func=ACT.Square,
+                    accum_out=square_sums[:, column : column + 1],
+                )
+            if m == TILES - 1:
+                nc.scalar.activation(
+                    out=rms[:], in_=square_sums[:], func=ACT.Sqrt, scale=1.0 / HEAD_DIM, bias=eps_column[:]
+                )
 
-        def finish_normed_and_rotated(n, banks):
+        def invert_rms(n):
+            nc.vector.reciprocal(out=norm_of[n][2][:], in_=norm_of[n][1][:])
+
+        def rotary_products(b):
+            n, m = divmod(b, TILES)
             straight, crossed = tables[units[n][2]]
-            result = result_pool.tile([P, POSITION_TILES, UNIT_COLS], F32, name="result")
-            cross_term = scratch_pool.tile([P, POSITION_TILES, UNIT_COLS], F32, name="cross_term")
-            squares = scratch_pool.tile([P, POSITION_TILES, UNIT_COLS], BF16, name="squares")
-            square_sums = scratch_pool.tile([P, POSITION_TILES * UNIT_HEADS], F32, name="square_sums")
-            rms = scratch_pool.tile([P, POSITION_TILES * UNIT_HEADS], F32, name="rms")
-            rinv = scratch_pool.tile([P, POSITION_TILES * UNIT_HEADS], F32, name="rinv")
-
-            for m in range(POSITION_TILES):
-                for h in range(UNIT_HEADS):
-                    head = slice(h * HEAD_DIM, (h + 1) * HEAD_DIM)
-                    column = m * UNIT_HEADS + h
-                    nc.scalar.activation(
-                        out=squares[:, m, head],
-                        in_=banks[m][:, head],
-                        func=ACT.Square,
-                        accum_out=square_sums[:, column : column + 1],
-                    )
-                u = banks[m][:].rearrange("p (h d) -> p h d", d=HEAD_DIM)
+            u = bank_of[b][:].rearrange("p (h d) -> p h d", d=HEAD_DIM)
+            result = result_pool.tile([P, UNIT_HEADS, HEAD_DIM], F32, name="result")
+            cross = scratch_pool.tile([P, UNIT_HEADS, HEAD_DIM], F32, name="cross")
+            nc.vector.tensor_tensor(
+                out=result[:],
+                in0=u,
+                in1=straight[:, m, :].unsqueeze(1).to_broadcast([P, UNIT_HEADS, HEAD_DIM]),
+                op=ALU.mult,
+            )
+            for here, there in ((low, high), (high, low)):
                 nc.vector.tensor_tensor(
-                    out=result[:, m, :].rearrange("p (h d) -> p h d", d=HEAD_DIM),
-                    in0=u,
-                    in1=straight[:, m, :].unsqueeze(1).to_broadcast([P, UNIT_HEADS, HEAD_DIM]),
+                    out=cross[:, :, here],
+                    in0=u[:, :, there],
+                    in1=crossed[:, m, here].unsqueeze(1).to_broadcast([P, UNIT_HEADS, HALF]),
                     op=ALU.mult,
                 )
-                cross = cross_term[:, m, :].rearrange("p (h d) -> p h d", d=HEAD_DIM)
-                for here, there in ((low, high), (high, low)):
-                    nc.vector.tensor_tensor(
-                        out=cross[:, :, here],
-                        in0=u[:, :, there],
-                        in1=crossed[:, m, here].unsqueeze(1).to_broadcast([P, UNIT_HEADS, HALF]),
-                        op=ALU.mult,
-                    )
+            result_of[b] = result
+            cross_of[b] = cross
 
-            nc.scalar.activation(
-                out=rms[:], in_=square_sums[:], func=ACT.Sqrt, scale=1.0 / HEAD_DIM, bias=eps_column[:]
-            )
-            nc.vector.reciprocal(out=rinv[:], in_=rms[:])
-            nc.vector.tensor_tensor(out=result[:], in0=result[:], in1=cross_term[:], op=ALU.add)
+        def add_products(b):
+            nc.vector.tensor_tensor(out=result_of[b][:], in0=result_of[b][:], in1=cross_of[b][:], op=ALU.add)
 
-            for m in range(POSITION_TILES):
-                for h in range(UNIT_HEADS):
-                    head = slice(h * HEAD_DIM, (h + 1) * HEAD_DIM)
-                    column = m * UNIT_HEADS + h
-                    nc.scalar.activation(
-                        out=result[:, m, head],
-                        in_=result[:, m, head],
-                        func=ACT.Copy,
-                        scale=rinv[:, column : column + 1],
-                    )
-                store(n, m, result)
+        def scale_and_store(b):
+            n, m = divmod(b, TILES)
+            rinv = norm_of[n][2]
+            for h in range(UNIT_HEADS):
+                column = m * UNIT_HEADS + h
+                nc.scalar.activation(
+                    out=result_of[b][:, h, :],
+                    in_=result_of[b][:, h, :],
+                    func=ACT.Copy,
+                    scale=rinv[:, column : column + 1],
+                )
+            store(b)
 
-        banks_of = {0: multiply_unit(0)}
-        for n in range(len(units)):
-            if n + UNITS_LOADED_AHEAD < len(units):
-                for g in range(PASSES):
-                    load_weight_chunk(n + UNITS_LOADED_AHEAD, g)
-            if n + 1 < len(units):
-                banks_of[n + 1] = multiply_unit(n + 1)
-            if units[n][2] is None:
-                finish_plain(n, banks_of[n])
-            else:
-                finish_normed_and_rotated(n, banks_of[n])
+        def copy_out_and_store(b):
+            result = result_pool.tile([P, UNIT_HEADS, HEAD_DIM], F32, name="result")
+            copy = nc.scalar.copy if b % 2 == 0 else nc.vector.tensor_copy
+            copy(out=result[:].rearrange("p h d -> p (h d)"), in_=bank_of[b][:])
+            result_of[b] = result
+            store(b)
+
+        def rotated(b):
+            return 0 <= b < banks and units[b // TILES][2] is not None
+
+        def plain(b):
+            return 0 <= b < banks and units[b // TILES][2] is None
+
+        def step(j):
+            if j % TILES == 0 and rotated(j - INVERT_AFTER):
+                invert_rms((j - INVERT_AFTER) // TILES)
+            if j + REGROUP_AHEAD < chunks:
+                regroup(j + REGROUP_AHEAD)
+            if rotated(j - PRODUCTS_AFTER):
+                rotary_products(j - PRODUCTS_AFTER)
+            if plain(j - PRODUCTS_AFTER):
+                copy_out_and_store(j - PRODUCTS_AFTER)
+            if j < chunks:
+                quantise_and_multiply(j)
+            if rotated(j - PRODUCTS_AFTER):
+                add_products(j - PRODUCTS_AFTER)
+            if rotated(j - SQUARES_AFTER):
+                sum_squares(j - SQUARES_AFTER)
+            if rotated(j - SCALE_AFTER):
+                scale_and_store(j - SCALE_AFTER)
+
+        x_tiles = []
+        for m in range(TILES):
+            load_chunk(m)
+            x_tile = const.tile([P, MODEL_DIM], BF16, name="x_tile%d" % m)
+            nc.sync.dma_start(out=x_tile[:], in_=x_rows[m * P : (m + 1) * P, :])
+            x_tiles.append(x_tile)
+        for j in range(PASSES, 2 * PASSES):
+            load_chunk(j)
+        cos_sb = const.tile([P, TILES, HEAD_DIM], BF16)
+        nc.sync.dma_start(out=cos_sb[:], in_=cos.rearrange("b s d -> (b s) d").rearrange("(m p) d -> p m d", p=P))
+        sin_sb = const.tile([P, TILES, HEAD_DIM], BF16)
+        nc.sync.dma_start(out=sin_sb[:], in_=sin.rearrange("b s d -> (b s) d").rearrange("(m p) d -> p m d", p=P))
+        q_gain = const.tile([P, HEAD_DIM], BF16)
+        nc.sync.dma_start(out=q_gain[:], in_=q_scale.partition_broadcast(P))
+        k_gain = const.tile([P, HEAD_DIM], BF16)
+        nc.sync.dma_start(out=k_gain[:], in_=k_scale.partition_broadcast(P))
+        for j in range(2 * PASSES, RAW_CHUNKS):
+            load_chunk(j)
+
+        identity = const.tile([P, P], F32)
+        make_identity(nc, identity[:])
+        eps_column = const.tile([P, 1], F32)
+        nc.vector.memset(eps_column[:], EPS)
+        x_words = const.tile([P, TILES, PASSES, P], U32, align_bytes=64)
+        x_scales = const.tile([P, TILES, PASSES, P], U8, align_bytes=64)
+
+        for m in range(TILES):
+            regroup(m)
+            turn_and_quantise_positions(m)
+        for j in range(PASSES):
+            step(j)
+        build_tables("q", q_gain)
+        build_tables("k", k_gain)
+        for j in range(PASSES, banks + SCALE_AFTER + 1):
+            step(j)

@@ -26,7 +26,7 @@ TILES = POSITIONS // P
 UNIT_COLS = 512
 UNIT_HEADS = UNIT_COLS // HEAD_DIM
 
-VECTOR_COLS = 208
+VECTOR_COLS = 288
 RUN = 4
 
 REGROUP_AHEAD = PASSES
@@ -226,7 +226,7 @@ def tile_multiheadattention_pa_kernel(
             cross_of[b] = cross
 
         def add_products(b):
-            nc.vector.tensor_tensor(out=result_of[b][:], in0=result_of[b][:], in1=cross_of[b][:], op=ALU.add)
+            nc.gpsimd.tensor_tensor(out=result_of[b][:], in0=result_of[b][:], in1=cross_of[b][:], op=ALU.add)
 
         def scale_and_store(b):
             n, m = divmod(b, TILES)

@@ -26,7 +26,7 @@ TILES = POSITIONS // P
 UNIT_COLS = 512
 UNIT_HEADS = UNIT_COLS // HEAD_DIM
 
-VECTOR_COLS = 288
+VECTOR_COLS = 272
 RUN = 4
 
 REGROUP_AHEAD = PASSES
@@ -71,7 +71,7 @@ def tile_multiheadattention_pa_kernel(
         grouped_of = {}
         bank_of = {}
         result_of = {}
-        cross_of = {}
+        partner_of = {}
         norm_of = {}
         tables = {}
 
@@ -145,36 +145,35 @@ def tile_multiheadattention_pa_kernel(
             )
 
         def build_tables(tables_name, gain_sb):
-            straight = const.tile([P, TILES, HEAD_DIM], F32, name="straight_" + tables_name)
-            crossed = const.tile([P, TILES, HEAD_DIM], F32, name="crossed_" + tables_name)
+            table = const.tile([P, TILES, 2, HEAD_DIM], F32, name="table_" + tables_name)
             nc.vector.tensor_tensor(
-                out=straight[:],
+                out=table[:, :, 0, :],
                 in0=cos_sb[:],
                 in1=gain_sb[:].unsqueeze(1).to_broadcast([P, TILES, HEAD_DIM]),
                 op=ALU.mult,
             )
+            nc.vector.tensor_tensor(
+                out=table[:, :, 1, low],
+                in0=sin_sb[:, :, high],
+                in1=gain_sb[:, low].unsqueeze(1).to_broadcast([P, TILES, HALF]),
+                op=ALU.mult,
+            )
             nc.vector.scalar_tensor_tensor(
-                out=crossed[:, :, low],
+                out=table[:, :, 1, high],
                 in0=sin_sb[:, :, low],
                 scalar=-1.0,
                 in1=gain_sb[:, high].unsqueeze(1).to_broadcast([P, TILES, HALF]),
                 op0=ALU.mult,
                 op1=ALU.mult,
             )
-            nc.vector.tensor_tensor(
-                out=crossed[:, :, high],
-                in0=sin_sb[:, :, high],
-                in1=gain_sb[:, low].unsqueeze(1).to_broadcast([P, TILES, HALF]),
-                op=ALU.mult,
-            )
-            tables[tables_name] = (straight, crossed)
+            tables[tables_name] = table
 
         def store(b):
             n, m = divmod(b, TILES)
             rows, first_col = units[n][1], units[n][3]
             nc.sync.dma_start(
                 out=rows[m * P : (m + 1) * P, first_col : first_col + UNIT_COLS],
-                in_=result_of[b][:].rearrange("p h d -> p (h d)"),
+                in_=result_of[b].rearrange("p h d -> p (h d)"),
             )
 
         def sum_squares(b):
@@ -205,28 +204,25 @@ def tile_multiheadattention_pa_kernel(
 
         def rotary_products(b):
             n, m = divmod(b, TILES)
-            straight, crossed = tables[units[n][2]]
-            u = bank_of[b][:].rearrange("p (h d) -> p h d", d=HEAD_DIM)
-            result = result_pool.tile([P, UNIT_HEADS, HEAD_DIM], F32, name="result")
-            cross = scratch_pool.tile([P, UNIT_HEADS, HEAD_DIM], F32, name="cross")
+            both_shape = [P, 2, UNIT_HEADS, HEAD_DIM]
+            products = result_pool.tile(both_shape, F32, name="products")
             nc.vector.tensor_tensor(
-                out=result[:],
-                in0=u,
-                in1=straight[:, m, :].unsqueeze(1).to_broadcast([P, UNIT_HEADS, HEAD_DIM]),
+                out=products[:],
+                in0=bank_of[b][:].rearrange("p (h d) -> p h d", d=HEAD_DIM).unsqueeze(1).to_broadcast(both_shape),
+                in1=tables[units[n][2]][:, m, :, :].unsqueeze(2).to_broadcast(both_shape),
                 op=ALU.mult,
             )
-            for here, there in ((low, high), (high, low)):
-                nc.vector.tensor_tensor(
-                    out=cross[:, :, here],
-                    in0=u[:, :, there],
-                    in1=crossed[:, m, here].unsqueeze(1).to_broadcast([P, UNIT_HEADS, HALF]),
-                    op=ALU.mult,
-                )
-            result_of[b] = result
-            cross_of[b] = cross
+            result_of[b] = products[:, 0, :, :]
+            partner_of[b] = products[:, 1, :, :]
 
         def add_products(b):
-            nc.gpsimd.tensor_tensor(out=result_of[b][:], in0=result_of[b][:], in1=cross_of[b][:], op=ALU.add)
+            for here, there in ((low, high), (high, low)):
+                nc.gpsimd.tensor_tensor(
+                    out=result_of[b][:, :, here],
+                    in0=result_of[b][:, :, here],
+                    in1=partner_of[b][:, :, there],
+                    op=ALU.add,
+                )
 
         def scale_and_store(b):
             n, m = divmod(b, TILES)
@@ -245,7 +241,7 @@ def tile_multiheadattention_pa_kernel(
             result = result_pool.tile([P, UNIT_HEADS, HEAD_DIM], F32, name="result")
             copy = nc.scalar.copy if b % 2 == 0 else nc.vector.tensor_copy
             copy(out=result[:].rearrange("p h d -> p (h d)"), in_=bank_of[b][:])
-            result_of[b] = result
+            result_of[b] = result[:]
             store(b)
 
         def rotated(b):

@@ -29,10 +29,13 @@ UNIT_HEADS = UNIT_COLS // HEAD_DIM
 VECTOR_COLS = 272
 RUN = 4
 
-REGROUP_AHEAD = PASSES
-SQUARES_AFTER = PASSES
+GROUP = 2
+UNIT_ROUNDS = PASSES // GROUP
+
+REGROUP_AHEAD = 1
+SQUARES_AFTER = UNIT_ROUNDS
 PRODUCTS_AFTER = SQUARES_AFTER + 1
-INVERT_AFTER = SQUARES_AFTER + TILES
+INVERT_AFTER = SQUARES_AFTER + UNIT_ROUNDS
 SCALE_AFTER = INVERT_AFTER + 1
 RAW_CHUNKS = 12
 
@@ -54,16 +57,16 @@ def tile_multiheadattention_pa_kernel(
         for first_col in range(0, weight.shape[1], UNIT_COLS):
             units.append((weight, rows, tables_name, first_col))
     chunks = len(units) * PASSES
-    banks = len(units) * TILES
+    groups = chunks // GROUP
 
     with ExitStack() as ctx:
         ctx.enter_context(tc.manual_schedule())
         const = ctx.enter_context(tc.tile_pool(name="const", bufs=1))
         x_stage = ctx.enter_context(tc.tile_pool(name="x_stage", bufs=2))
         raw_pool = ctx.enter_context(tc.tile_pool(name="raw", bufs=RAW_CHUNKS))
-        grouped_pool = ctx.enter_context(tc.tile_pool(name="grouped", bufs=REGROUP_AHEAD + 2))
+        grouped_pool = ctx.enter_context(tc.tile_pool(name="grouped", bufs=3 * GROUP))
         packed_pool = ctx.enter_context(tc.tile_pool(name="packed", bufs=2 * PASSES))
-        result_pool = ctx.enter_context(tc.tile_pool(name="result", bufs=SCALE_AFTER - PRODUCTS_AFTER + 4))
+        result_pool = ctx.enter_context(tc.tile_pool(name="result", bufs=SCALE_AFTER - PRODUCTS_AFTER + 3))
         scratch_pool = ctx.enter_context(tc.tile_pool(name="scratch", bufs=3))
         psum = ctx.enter_context(tc.psum_pool(name="psum", bufs=8))
 
@@ -71,9 +74,18 @@ def tile_multiheadattention_pa_kernel(
         grouped_of = {}
         bank_of = {}
         result_of = {}
-        partner_of = {}
+        cross_of = {}
         norm_of = {}
         tables = {}
+
+        def members(r):
+            return range(r * GROUP, (r + 1) * GROUP)
+
+        def rotated(r):
+            return 0 <= r < groups and units[r // UNIT_ROUNDS][2] is not None
+
+        def plain(r):
+            return 0 <= r < groups and units[r // UNIT_ROUNDS][2] is None
 
         def load_chunk(j):
             n, g = divmod(j, PASSES)
@@ -145,35 +157,36 @@ def tile_multiheadattention_pa_kernel(
             )
 
         def build_tables(tables_name, gain_sb):
-            table = const.tile([P, TILES, 2, HEAD_DIM], F32, name="table_" + tables_name)
+            straight = const.tile([P, TILES, HEAD_DIM], F32, name="straight_" + tables_name)
+            crossed = const.tile([P, TILES, HEAD_DIM], F32, name="crossed_" + tables_name)
             nc.vector.tensor_tensor(
-                out=table[:, :, 0, :],
+                out=straight[:],
                 in0=cos_sb[:],
                 in1=gain_sb[:].unsqueeze(1).to_broadcast([P, TILES, HEAD_DIM]),
                 op=ALU.mult,
             )
-            nc.vector.tensor_tensor(
-                out=table[:, :, 1, low],
-                in0=sin_sb[:, :, high],
-                in1=gain_sb[:, low].unsqueeze(1).to_broadcast([P, TILES, HALF]),
-                op=ALU.mult,
-            )
             nc.vector.scalar_tensor_tensor(
-                out=table[:, :, 1, high],
+                out=crossed[:, :, low],
                 in0=sin_sb[:, :, low],
                 scalar=-1.0,
                 in1=gain_sb[:, high].unsqueeze(1).to_broadcast([P, TILES, HALF]),
                 op0=ALU.mult,
                 op1=ALU.mult,
             )
-            tables[tables_name] = table
+            nc.vector.tensor_tensor(
+                out=crossed[:, :, high],
+                in0=sin_sb[:, :, high],
+                in1=gain_sb[:, low].unsqueeze(1).to_broadcast([P, TILES, HALF]),
+                op=ALU.mult,
+            )
+            tables[tables_name] = (straight, crossed)
 
         def store(b):
             n, m = divmod(b, TILES)
             rows, first_col = units[n][1], units[n][3]
             nc.sync.dma_start(
                 out=rows[m * P : (m + 1) * P, first_col : first_col + UNIT_COLS],
-                in_=result_of[b].rearrange("p h d -> p (h d)"),
+                in_=result_of[b // GROUP][:, b % GROUP, :, :].rearrange("p h d -> p (h d)"),
             )
 
         def sum_squares(b):
@@ -202,27 +215,31 @@ def tile_multiheadattention_pa_kernel(
         def invert_rms(n):
             nc.vector.reciprocal(out=norm_of[n][2][:], in_=norm_of[n][1][:])
 
-        def rotary_products(b):
-            n, m = divmod(b, TILES)
-            both_shape = [P, 2, UNIT_HEADS, HEAD_DIM]
-            products = result_pool.tile(both_shape, F32, name="products")
-            nc.vector.tensor_tensor(
-                out=products[:],
-                in0=bank_of[b][:].rearrange("p (h d) -> p h d", d=HEAD_DIM).unsqueeze(1).to_broadcast(both_shape),
-                in1=tables[units[n][2]][:, m, :, :].unsqueeze(2).to_broadcast(both_shape),
-                op=ALU.mult,
-            )
-            result_of[b] = products[:, 0, :, :]
-            partner_of[b] = products[:, 1, :, :]
-
-        def add_products(b):
-            for here, there in ((low, high), (high, low)):
-                nc.gpsimd.tensor_tensor(
-                    out=result_of[b][:, :, here],
-                    in0=result_of[b][:, :, here],
-                    in1=partner_of[b][:, :, there],
-                    op=ALU.add,
+        def rotary_products(r):
+            result = result_pool.tile([P, GROUP, UNIT_HEADS, HEAD_DIM], F32, name="result")
+            cross = scratch_pool.tile([P, GROUP, UNIT_HEADS, HEAD_DIM], F32, name="cross")
+            for i, b in enumerate(members(r)):
+                n, m = divmod(b, TILES)
+                straight, crossed = tables[units[n][2]]
+                u = bank_of[b][:].rearrange("p (h d) -> p h d", d=HEAD_DIM)
+                nc.vector.tensor_tensor(
+                    out=result[:, i, :, :],
+                    in0=u,
+                    in1=straight[:, m, :].unsqueeze(1).to_broadcast([P, UNIT_HEADS, HEAD_DIM]),
+                    op=ALU.mult,
                 )
+                for here, there in ((low, high), (high, low)):
+                    nc.vector.tensor_tensor(
+                        out=cross[:, i, :, here],
+                        in0=u[:, :, there],
+                        in1=crossed[:, m, here].unsqueeze(1).to_broadcast([P, UNIT_HEADS, HALF]),
+                        op=ALU.mult,
+                    )
+            result_of[r] = result
+            cross_of[r] = cross
+
+        def add_products(r):
+            nc.gpsimd.tensor_tensor(out=result_of[r][:], in0=result_of[r][:], in1=cross_of[r][:], op=ALU.add)
 
         def scale_and_store(b):
             n, m = divmod(b, TILES)
@@ -230,43 +247,43 @@ def tile_multiheadattention_pa_kernel(
             for h in range(UNIT_HEADS):
                 column = m * UNIT_HEADS + h
                 nc.scalar.activation(
-                    out=result_of[b][:, h, :],
-                    in_=result_of[b][:, h, :],
+                    out=result_of[b // GROUP][:, b % GROUP, h, :],
+                    in_=result_of[b // GROUP][:, b % GROUP, h, :],
                     func=ACT.Copy,
                     scale=rinv[:, column : column + 1],
                 )
             store(b)
 
-        def copy_out_and_store(b):
-            result = result_pool.tile([P, UNIT_HEADS, HEAD_DIM], F32, name="result")
-            copy = nc.scalar.copy if b % 2 == 0 else nc.vector.tensor_copy
-            copy(out=result[:].rearrange("p h d -> p (h d)"), in_=bank_of[b][:])
-            result_of[b] = result[:]
-            store(b)
+        def copy_out_and_store(r):
+            result = result_pool.tile([P, GROUP, UNIT_HEADS, HEAD_DIM], F32, name="result")
+            result_of[r] = result
+            for i, b in enumerate(members(r)):
+                copy = nc.scalar.copy if b % 2 == 0 else nc.vector.tensor_copy
+                copy(out=result[:, i, :, :].rearrange("p h d -> p (h d)"), in_=bank_of[b][:])
+                store(b)
 
-        def rotated(b):
-            return 0 <= b < banks and units[b // TILES][2] is not None
-
-        def plain(b):
-            return 0 <= b < banks and units[b // TILES][2] is None
-
-        def step(j):
-            if j % TILES == 0 and rotated(j - INVERT_AFTER):
-                invert_rms((j - INVERT_AFTER) // TILES)
-            if j + REGROUP_AHEAD < chunks:
-                regroup(j + REGROUP_AHEAD)
-            if rotated(j - PRODUCTS_AFTER):
-                rotary_products(j - PRODUCTS_AFTER)
-            if plain(j - PRODUCTS_AFTER):
-                copy_out_and_store(j - PRODUCTS_AFTER)
-            if j < chunks:
-                quantise_and_multiply(j)
-            if rotated(j - PRODUCTS_AFTER):
-                add_products(j - PRODUCTS_AFTER)
-            if rotated(j - SQUARES_AFTER):
-                sum_squares(j - SQUARES_AFTER)
-            if rotated(j - SCALE_AFTER):
-                scale_and_store(j - SCALE_AFTER)
+        def do_round(r):
+            if (r - INVERT_AFTER) % UNIT_ROUNDS == 0 and rotated(r - INVERT_AFTER):
+                invert_rms((r - INVERT_AFTER) // UNIT_ROUNDS)
+            if rotated(r - PRODUCTS_AFTER):
+                rotary_products(r - PRODUCTS_AFTER)
+                add_products(r - PRODUCTS_AFTER)
+            if r + REGROUP_AHEAD < groups:
+                for j in members(r + REGROUP_AHEAD):
+                    regroup(j)
+                    if j < TILES:
+                        turn_and_quantise_positions(j)
+            if 0 <= r < groups:
+                for j in members(r):
+                    quantise_and_multiply(j)
+            if plain(r - PRODUCTS_AFTER):
+                copy_out_and_store(r - PRODUCTS_AFTER)
+            if rotated(r - SQUARES_AFTER):
+                for b in members(r - SQUARES_AFTER):
+                    sum_squares(b)
+            if rotated(r - SCALE_AFTER):
+                for b in members(r - SCALE_AFTER):
+                    scale_and_store(b)
 
         x_tiles = []
         for m in range(TILES):
@@ -294,12 +311,9 @@ def tile_multiheadattention_pa_kernel(
         x_words = const.tile([P, TILES, PASSES, P], U32, align_bytes=64)
         x_scales = const.tile([P, TILES, PASSES, P], U8, align_bytes=64)
 
-        for m in range(TILES):
-            regroup(m)
-            turn_and_quantise_positions(m)
-        for j in range(PASSES):
-            step(j)
+        for r in range(-REGROUP_AHEAD, PRODUCTS_AFTER):
+            do_round(r)
         build_tables("q", q_gain)
         build_tables("k", k_gain)
-        for j in range(PASSES, banks + SCALE_AFTER + 1):
-            step(j)
+        for r in range(PRODUCTS_AFTER, groups + SCALE_AFTER + 1):
+            do_round(r)

@@ -26,7 +26,8 @@ TILES = POSITIONS // P
 UNIT_COLS = 512
 UNIT_HEADS = UNIT_COLS // HEAD_DIM
 
-VECTOR_COLS = 272
+HEAD_VECTOR_COLS = 240
+VECTOR_COLS = 160
 RUN = 4
 
 GROUP = 2
@@ -35,8 +36,7 @@ UNIT_ROUNDS = PASSES // GROUP
 REGROUP_AHEAD = 1
 SQUARES_AFTER = UNIT_ROUNDS
 PRODUCTS_AFTER = SQUARES_AFTER + 1
-INVERT_AFTER = SQUARES_AFTER + UNIT_ROUNDS
-SCALE_AFTER = INVERT_AFTER + 1
+STORE_AFTER = PRODUCTS_AFTER + 1
 RAW_CHUNKS = 12
 
 FLOPS = 2 * POSITIONS * MODEL_DIM * (2048 + 1024 + 1024)
@@ -66,7 +66,7 @@ def tile_multiheadattention_pa_kernel(
         raw_pool = ctx.enter_context(tc.tile_pool(name="raw", bufs=RAW_CHUNKS))
         grouped_pool = ctx.enter_context(tc.tile_pool(name="grouped", bufs=3 * GROUP))
         packed_pool = ctx.enter_context(tc.tile_pool(name="packed", bufs=2 * PASSES))
-        result_pool = ctx.enter_context(tc.tile_pool(name="result", bufs=SCALE_AFTER - PRODUCTS_AFTER + 3))
+        result_pool = ctx.enter_context(tc.tile_pool(name="result", bufs=5))
         scratch_pool = ctx.enter_context(tc.tile_pool(name="scratch", bufs=3))
         psum = ctx.enter_context(tc.psum_pool(name="psum", bufs=8))
 
@@ -74,8 +74,8 @@ def tile_multiheadattention_pa_kernel(
         grouped_of = {}
         bank_of = {}
         result_of = {}
-        cross_of = {}
         norm_of = {}
+        packed_of = {}
         tables = {}
 
         def members(r):
@@ -102,20 +102,20 @@ def tile_multiheadattention_pa_kernel(
         def regroup(j):
             raw = raw_of[j]
             grouped = grouped_pool.tile([P, UNIT_COLS, PACK], BF16, align_bytes=64, name="grouped")
+            vector_cols = HEAD_VECTOR_COLS if j // GROUP - REGROUP_AHEAD < SQUARES_AFTER else VECTOR_COLS
             nc.vector.tensor_copy(
-                out=grouped[:, :VECTOR_COLS, :].rearrange("p (c i) t -> p c t i", i=RUN),
-                in_=raw[:, :, :VECTOR_COLS].rearrange("p t (c i) -> p c t i", i=RUN),
+                out=grouped[:, :vector_cols, :].rearrange("p (c i) t -> p c t i", i=RUN),
+                in_=raw[:, :, :vector_cols].rearrange("p t (c i) -> p c t i", i=RUN),
             )
             nc.scalar.copy(
-                out=grouped[:, VECTOR_COLS:, :].rearrange("p (c i) t -> p c t i", i=RUN),
-                in_=raw[:, :, VECTOR_COLS:].rearrange("p t (c i) -> p c t i", i=RUN),
+                out=grouped[:, vector_cols:, :].rearrange("p (c i) t -> p c t i", i=RUN),
+                in_=raw[:, :, vector_cols:].rearrange("p t (c i) -> p c t i", i=RUN),
             )
             grouped_of[j] = grouped
             if j + RAW_CHUNKS < chunks:
                 load_chunk(j + RAW_CHUNKS)
 
-        def quantise_and_multiply(j):
-            n, g = divmod(j, PASSES)
+        def quantise(j):
             w_words = packed_pool.tile([P, UNIT_COLS], U32, align_bytes=64, name="w_words")
             w_scales = packed_pool.tile([P, UNIT_COLS], U8, align_bytes=64, name="w_scales")
             nc.vector.quantize_mx(
@@ -123,6 +123,11 @@ def tile_multiheadattention_pa_kernel(
                 scales=w_scales[:],
                 in_=grouped_of[j][:].rearrange("p c t -> p (c t)"),
             )
+            packed_of[j] = (w_words, w_scales)
+
+        def multiply(j):
+            n, g = divmod(j, PASSES)
+            w_words, w_scales = packed_of[j]
             for m in range(TILES):
                 b = n * TILES + m
                 if g == 0:
@@ -189,70 +194,61 @@ def tile_multiheadattention_pa_kernel(
                 in_=result_of[b // GROUP][:, b % GROUP, :, :].rearrange("p h d -> p (h d)"),
             )
 
-        def sum_squares(b):
-            n, m = divmod(b, TILES)
-            if m == 0:
-                norm_of[n] = [
-                    scratch_pool.tile([P, TILES * UNIT_HEADS], F32, name=name)
-                    for name in ("square_sums", "rms", "rinv")
-                ]
-            square_sums, rms = norm_of[n][0], norm_of[n][1]
-            squares = scratch_pool.tile([P, UNIT_COLS], BF16, name="squares")
-            for h in range(UNIT_HEADS):
-                head = slice(h * HEAD_DIM, (h + 1) * HEAD_DIM)
-                column = m * UNIT_HEADS + h
-                nc.scalar.activation(
-                    out=squares[:, head],
-                    in_=bank_of[b][:, head],
-                    func=ACT.Square,
-                    accum_out=square_sums[:, column : column + 1],
-                )
-            if m == TILES - 1:
-                nc.scalar.activation(
-                    out=rms[:], in_=square_sums[:], func=ACT.Sqrt, scale=1.0 / HEAD_DIM, bias=eps_column[:]
-                )
+        def sum_squares(r):
+            square_sums = scratch_pool.tile([P, GROUP * UNIT_HEADS], F32, name="square_sums")
+            rinv = scratch_pool.tile([P, GROUP * UNIT_HEADS], F32, name="rinv")
+            norm_of[r] = (square_sums, rinv)
+            for i, b in enumerate(members(r)):
+                squares = scratch_pool.tile([P, UNIT_COLS], BF16, name="squares")
+                for h in range(UNIT_HEADS):
+                    head = slice(h * HEAD_DIM, (h + 1) * HEAD_DIM)
+                    column = i * UNIT_HEADS + h
+                    nc.scalar.activation(
+                        out=squares[:, head],
+                        in_=bank_of[b][:, head],
+                        func=ACT.Square,
+                        accum_out=square_sums[:, column : column + 1],
+                    )
 
-        def invert_rms(n):
-            nc.vector.reciprocal(out=norm_of[n][2][:], in_=norm_of[n][1][:])
+        def invert_rms(r):
+            square_sums, rinv = norm_of[r]
+            nc.scalar.activation(
+                out=rinv[:],
+                in_=square_sums[:],
+                func=ACT.Abs_reciprocal_sqrt,
+                scale=1.0 / HEAD_DIM,
+                bias=eps_column[:],
+            )
 
         def rotary_products(r):
+            rinv = norm_of[r][1]
             result = result_pool.tile([P, GROUP, UNIT_HEADS, HEAD_DIM], F32, name="result")
             cross = scratch_pool.tile([P, GROUP, UNIT_HEADS, HEAD_DIM], F32, name="cross")
             for i, b in enumerate(members(r)):
                 n, m = divmod(b, TILES)
                 straight, crossed = tables[units[n][2]]
                 u = bank_of[b][:].rearrange("p (h d) -> p h d", d=HEAD_DIM)
-                nc.vector.tensor_tensor(
-                    out=result[:, i, :, :],
-                    in0=u,
-                    in1=straight[:, m, :].unsqueeze(1).to_broadcast([P, UNIT_HEADS, HEAD_DIM]),
-                    op=ALU.mult,
-                )
-                for here, there in ((low, high), (high, low)):
-                    nc.vector.tensor_tensor(
-                        out=cross[:, i, :, here],
-                        in0=u[:, :, there],
-                        in1=crossed[:, m, here].unsqueeze(1).to_broadcast([P, UNIT_HEADS, HALF]),
-                        op=ALU.mult,
+                for h in range(UNIT_HEADS):
+                    column = i * UNIT_HEADS + h
+                    nc.vector.scalar_tensor_tensor(
+                        out=result[:, i, h, :],
+                        in0=u[:, h, :],
+                        scalar=rinv[:, column : column + 1],
+                        in1=straight[:, m, :],
+                        op0=ALU.mult,
+                        op1=ALU.mult,
                     )
+                    for here, there in ((low, high), (high, low)):
+                        nc.vector.scalar_tensor_tensor(
+                            out=cross[:, i, h, here],
+                            in0=u[:, h, there],
+                            scalar=rinv[:, column : column + 1],
+                            in1=crossed[:, m, here],
+                            op0=ALU.mult,
+                            op1=ALU.mult,
+                        )
             result_of[r] = result
-            cross_of[r] = cross
-
-        def add_products(r):
-            nc.gpsimd.tensor_tensor(out=result_of[r][:], in0=result_of[r][:], in1=cross_of[r][:], op=ALU.add)
-
-        def scale_and_store(b):
-            n, m = divmod(b, TILES)
-            rinv = norm_of[n][2]
-            for h in range(UNIT_HEADS):
-                column = m * UNIT_HEADS + h
-                nc.scalar.activation(
-                    out=result_of[b // GROUP][:, b % GROUP, h, :],
-                    in_=result_of[b // GROUP][:, b % GROUP, h, :],
-                    func=ACT.Copy,
-                    scale=rinv[:, column : column + 1],
-                )
-            store(b)
+            nc.gpsimd.tensor_tensor(out=result[:], in0=result[:], in1=cross[:], op=ALU.add)
 
         def copy_out_and_store(r):
             result = result_pool.tile([P, GROUP, UNIT_HEADS, HEAD_DIM], F32, name="result")
@@ -263,11 +259,8 @@ def tile_multiheadattention_pa_kernel(
                 store(b)
 
         def do_round(r):
-            if (r - INVERT_AFTER) % UNIT_ROUNDS == 0 and rotated(r - INVERT_AFTER):
-                invert_rms((r - INVERT_AFTER) // UNIT_ROUNDS)
             if rotated(r - PRODUCTS_AFTER):
-                rotary_products(r - PRODUCTS_AFTER)
-                add_products(r - PRODUCTS_AFTER)
+                invert_rms(r - PRODUCTS_AFTER)
             if r + REGROUP_AHEAD < groups:
                 for j in members(r + REGROUP_AHEAD):
                     regroup(j)
@@ -275,15 +268,19 @@ def tile_multiheadattention_pa_kernel(
                         turn_and_quantise_positions(j)
             if 0 <= r < groups:
                 for j in members(r):
-                    quantise_and_multiply(j)
+                    quantise(j)
+            if rotated(r - PRODUCTS_AFTER):
+                rotary_products(r - PRODUCTS_AFTER)
+            if 0 <= r < groups:
+                for j in members(r):
+                    multiply(j)
             if plain(r - PRODUCTS_AFTER):
                 copy_out_and_store(r - PRODUCTS_AFTER)
             if rotated(r - SQUARES_AFTER):
-                for b in members(r - SQUARES_AFTER):
-                    sum_squares(b)
-            if rotated(r - SCALE_AFTER):
-                for b in members(r - SCALE_AFTER):
-                    scale_and_store(b)
+                sum_squares(r - SQUARES_AFTER)
+            if rotated(r - STORE_AFTER):
+                for b in members(r - STORE_AFTER):
+                    store(b)
 
         x_tiles = []
         for m in range(TILES):
@@ -315,5 +312,5 @@ def tile_multiheadattention_pa_kernel(
             do_round(r)
         build_tables("q", q_gain)
         build_tables("k", k_gain)
-        for r in range(PRODUCTS_AFTER, groups + SCALE_AFTER + 1):
+        for r in range(PRODUCTS_AFTER, groups + PRODUCTS_AFTER):
             do_round(r)

@@ -27,7 +27,7 @@ UNIT_COLS = 512
 UNIT_HEADS = UNIT_COLS // HEAD_DIM
 
 HEAD_VECTOR_COLS = 240
-VECTOR_COLS = 160
+VECTOR_COLS = 192
 RUN = 4
 
 GROUP = 2

@@ -26,8 +26,8 @@ TILES = POSITIONS // P
 UNIT_COLS = 512
 UNIT_HEADS = UNIT_COLS // HEAD_DIM
 
-HEAD_VECTOR_COLS = 240
-VECTOR_COLS = 192
+VECTOR_COLS = {(False, False): 256, (True, False): 352, (True, True): 176, (False, True): 80}
+FIRST_UNIT_VECTOR_COLS = 176
 RUN = 4
 
 GROUP = 2
@@ -102,7 +102,10 @@ def tile_multiheadattention_pa_kernel(
         def regroup(j):
             raw = raw_of[j]
             grouped = grouped_pool.tile([P, UNIT_COLS, PACK], BF16, align_bytes=64, name="grouped")
-            vector_cols = HEAD_VECTOR_COLS if j // GROUP - REGROUP_AHEAD < SQUARES_AFTER else VECTOR_COLS
+            r = j // GROUP - REGROUP_AHEAD
+            vector_cols = VECTOR_COLS[(rotated(r - SQUARES_AFTER), rotated(r - PRODUCTS_AFTER))]
+            if j < PASSES:
+                vector_cols = FIRST_UNIT_VECTOR_COLS
             nc.vector.tensor_copy(
                 out=grouped[:, :vector_cols, :].rearrange("p (c i) t -> p c t i", i=RUN),
                 in_=raw[:, :, :vector_cols].rearrange("p t (c i) -> p c t i", i=RUN),
@@ -264,14 +267,12 @@ def tile_multiheadattention_pa_kernel(
             if r + REGROUP_AHEAD < groups:
                 for j in members(r + REGROUP_AHEAD):
                     regroup(j)
-                    if j < TILES:
-                        turn_and_quantise_positions(j)
-            if 0 <= r < groups:
+            if UNIT_ROUNDS <= r < groups:
                 for j in members(r):
                     quantise(j)
             if rotated(r - PRODUCTS_AFTER):
                 rotary_products(r - PRODUCTS_AFTER)
-            if 0 <= r < groups:
+            if UNIT_ROUNDS <= r < groups:
                 for j in members(r):
                     multiply(j)
             if plain(r - PRODUCTS_AFTER):
@@ -305,10 +306,20 @@ def tile_multiheadattention_pa_kernel(
         make_identity(nc, identity[:])
         eps_column = const.tile([P, 1], F32)
         nc.vector.memset(eps_column[:], EPS)
+        warm_up = const.tile([P, 1], F32)
+        nc.scalar.activation(out=warm_up[:], in_=eps_column[:], func=ACT.Abs_reciprocal_sqrt)
         x_words = const.tile([P, TILES, PASSES, P], U32, align_bytes=64)
         x_scales = const.tile([P, TILES, PASSES, P], U8, align_bytes=64)
 
-        for r in range(-REGROUP_AHEAD, PRODUCTS_AFTER):
+        for j in range(PASSES):
+            regroup(j)
+            if j > 0:
+                turn_and_quantise_positions(j - 1)
+            quantise(j)
+        turn_and_quantise_positions(TILES - 1)
+        for j in range(PASSES):
+            multiply(j)
+        for r in range(UNIT_ROUNDS - REGROUP_AHEAD, PRODUCTS_AFTER):
             do_round(r)
         build_tables("q", q_gain)
         build_tables("k", k_gain)

@@ -26,7 +26,7 @@ TILES = POSITIONS // P
 UNIT_COLS = 512
 UNIT_HEADS = UNIT_COLS // HEAD_DIM
 
-VECTOR_COLS = {(False, False): 256, (True, False): 352, (True, True): 176, (False, True): 80}
+VECTOR_COLS = {(False, False): 256, (True, False): 352, (True, True): 192, (False, True): 80}
 FIRST_UNIT_VECTOR_COLS = 176
 RUN = 4
 
@@ -241,15 +241,14 @@ def tile_multiheadattention_pa_kernel(
                         op0=ALU.mult,
                         op1=ALU.mult,
                     )
-                    for here, there in ((low, high), (high, low)):
-                        nc.vector.scalar_tensor_tensor(
-                            out=cross[:, i, h, here],
-                            in0=u[:, h, there],
-                            scalar=rinv[:, column : column + 1],
-                            in1=crossed[:, m, here],
-                            op0=ALU.mult,
-                            op1=ALU.mult,
-                        )
+                    nc.vector.scalar_tensor_tensor(
+                        out=cross[:, i, h, :].rearrange("p (two d) -> p two d", two=2),
+                        in0=u[:, h, :].rearrange("p (two d) -> p two d", two=2)[:, ::-1, :],
+                        scalar=rinv[:, column : column + 1],
+                        in1=crossed[:, m, :].rearrange("p (two d) -> p two d", two=2),
+                        op0=ALU.mult,
+                        op1=ALU.mult,
+                    )
             result_of[r] = result
             nc.gpsimd.tensor_tensor(out=result[:], in0=result[:], in1=cross[:], op=ALU.add)
 

@@ -26,7 +26,7 @@ TILES = POSITIONS // P
 UNIT_COLS = 512
 UNIT_HEADS = UNIT_COLS // HEAD_DIM
 
-VECTOR_COLS = {(False, False): 256, (True, False): 352, (True, True): 192, (False, True): 80}
+VECTOR_COLS = {(False, False): 256, (True, False): 352, (True, True): 200, (False, True): 80}
 FIRST_UNIT_VECTOR_COLS = 176
 RUN = 4
 
@@ -165,29 +165,24 @@ def tile_multiheadattention_pa_kernel(
             )
 
         def build_tables(tables_name, gain_sb):
-            straight = const.tile([P, TILES, HEAD_DIM], F32, name="straight_" + tables_name)
-            crossed = const.tile([P, TILES, HEAD_DIM], F32, name="crossed_" + tables_name)
-            nc.vector.tensor_tensor(
-                out=straight[:],
-                in0=cos_sb[:],
-                in1=gain_sb[:].unsqueeze(1).to_broadcast([P, TILES, HEAD_DIM]),
-                op=ALU.mult,
-            )
+            table = const.tile([P, TILES, 2, HEAD_DIM], F32, name="table_" + tables_name)
+            for j, half, trig in ((0, low, cos_sb), (1, low, sin_sb), (1, high, cos_sb)):
+                source = low if j == 0 else high
+                nc.vector.tensor_tensor(
+                    out=table[:, :, j, half],
+                    in0=trig[:, :, source],
+                    in1=gain_sb[:, half].unsqueeze(1).to_broadcast([P, TILES, HALF]),
+                    op=ALU.mult,
+                )
             nc.vector.scalar_tensor_tensor(
-                out=crossed[:, :, low],
+                out=table[:, :, 0, high],
                 in0=sin_sb[:, :, low],
                 scalar=-1.0,
                 in1=gain_sb[:, high].unsqueeze(1).to_broadcast([P, TILES, HALF]),
                 op0=ALU.mult,
                 op1=ALU.mult,
             )
-            nc.vector.tensor_tensor(
-                out=crossed[:, :, high],
-                in0=sin_sb[:, :, high],
-                in1=gain_sb[:, low].unsqueeze(1).to_broadcast([P, TILES, HALF]),
-                op=ALU.mult,
-            )
-            tables[tables_name] = (straight, crossed)
+            tables[tables_name] = table
 
         def store(b):
             n, m = divmod(b, TILES)
@@ -226,31 +221,28 @@ def tile_multiheadattention_pa_kernel(
         def rotary_products(r):
             rinv = norm_of[r][1]
             result = result_pool.tile([P, GROUP, UNIT_HEADS, HEAD_DIM], F32, name="result")
-            cross = scratch_pool.tile([P, GROUP, UNIT_HEADS, HEAD_DIM], F32, name="cross")
+            products = scratch_pool.tile([P, GROUP, UNIT_HEADS, 2, HEAD_DIM], F32, name="products")
             for i, b in enumerate(members(r)):
                 n, m = divmod(b, TILES)
-                straight, crossed = tables[units[n][2]]
                 u = bank_of[b][:].rearrange("p (h d) -> p h d", d=HEAD_DIM)
                 for h in range(UNIT_HEADS):
                     column = i * UNIT_HEADS + h
                     nc.vector.scalar_tensor_tensor(
-                        out=result[:, i, h, :],
-                        in0=u[:, h, :],
+                        out=products[:, i, h, :, :],
+                        in0=u[:, h, :].unsqueeze(1).to_broadcast([P, 2, HEAD_DIM]),
                         scalar=rinv[:, column : column + 1],
-                        in1=straight[:, m, :],
-                        op0=ALU.mult,
-                        op1=ALU.mult,
-                    )
-                    nc.vector.scalar_tensor_tensor(
-                        out=cross[:, i, h, :].rearrange("p (two d) -> p two d", two=2),
-                        in0=u[:, h, :].rearrange("p (two d) -> p two d", two=2)[:, ::-1, :],
-                        scalar=rinv[:, column : column + 1],
-                        in1=crossed[:, m, :].rearrange("p (two d) -> p two d", two=2),
+                        in1=tables[units[n][2]][:, m, :, :],
                         op0=ALU.mult,
                         op1=ALU.mult,
                     )
             result_of[r] = result
-            nc.gpsimd.tensor_tensor(out=result[:], in0=result[:], in1=cross[:], op=ALU.add)
+            halves = products[:].rearrange("p i h j (two e) -> p (i h j) two e", two=2)
+            nc.gpsimd.tensor_tensor(
+                out=result[:].rearrange("p i h (j e) -> p (i h j) e", j=2),
+                in0=halves[:, :, 0, :],
+                in1=halves[:, :, 1, :],
+                op=ALU.add,
+            )
 
         def copy_out_and_store(r):
             result = result_pool.tile([P, GROUP, UNIT_HEADS, HEAD_DIM], F32, name="result")

from contextlib import ExitStack

import concourse.mybir as mybir
from concourse.masks import make_identity

F32 = mybir.dt.float32
BF16 = mybir.dt.bfloat16
U32 = mybir.dt.uint32
U8 = mybir.dt.uint8
FP8X4 = mybir.dt.float8_e4m3fn_x4
ACT = mybir.ActivationFunctionType
ALU = mybir.AluOpType

P = 128
PACK = 4
PAIRS = PACK // 2
K_PASS = P * PACK
POSITIONS = 512
MODEL_DIM = 2048
HEAD_DIM = 128
HALF = HEAD_DIM // 2
EPS = 1e-6

PASSES = MODEL_DIM // K_PASS
TILES = POSITIONS // P
UNIT_COLS = 512
UNIT_HEADS = UNIT_COLS // HEAD_DIM

VECTOR_COLS = {(False, False): 256, (True, False): 352, (True, True): 200, (False, True): 80}
FIRST_UNIT_VECTOR_COLS = 176
RUN = 4

GROUP = 2
UNIT_ROUNDS = PASSES // GROUP

REGROUP_AHEAD = 1
SQUARES_AFTER = UNIT_ROUNDS
PRODUCTS_AFTER = SQUARES_AFTER + 1
STORE_AFTER = PRODUCTS_AFTER + 1
RAW_CHUNKS = 12

FLOPS = 2 * POSITIONS * MODEL_DIM * (2048 + 1024 + 1024)


def tile_multiheadattention_pa_kernel(
    tc, hidden_states, cos, sin, Wq, Wk, Wv, q_scale, k_scale, out_0, out_1, out_2
):
    nc = tc.nc
    x_rows = hidden_states.rearrange("b s k -> (b s) k")
    q_rows = out_0.rearrange("b s h d -> (b s) (h d)")
    k_rows = out_1.rearrange("b s h d -> (b s) (h d)")
    v_rows = out_2.rearrange("b s h d -> (b s) (h d)")
    low, high = slice(0, HALF), slice(HALF, HEAD_DIM)

    units = []
    for weight, rows, tables_name in ((Wq, q_rows, "q"), (Wk, k_rows, "k"), (Wv, v_rows, None)):
        for first_col in range(0, weight.shape[1], UNIT_COLS):
            units.append((weight, rows, tables_name, first_col))
    chunks = len(units) * PASSES
    groups = chunks // GROUP

    with ExitStack() as ctx:
        ctx.enter_context(tc.manual_schedule())
        const = ctx.enter_context(tc.tile_pool(name="const", bufs=1))
        x_stage = ctx.enter_context(tc.tile_pool(name="x_stage", bufs=2))
        raw_pool = ctx.enter_context(tc.tile_pool(name="raw", bufs=RAW_CHUNKS))
        grouped_pool = ctx.enter_context(tc.tile_pool(name="grouped", bufs=3 * GROUP))
        packed_pool = ctx.enter_context(tc.tile_pool(name="packed", bufs=2 * PASSES))
        result_pool = ctx.enter_context(tc.tile_pool(name="result", bufs=5))
        scratch_pool = ctx.enter_context(tc.tile_pool(name="scratch", bufs=3))
        psum = ctx.enter_context(tc.psum_pool(name="psum", bufs=8))

        raw_of = {}
        grouped_of = {}
        bank_of = {}
        result_of = {}
        norm_of = {}
        packed_of = {}
        tables = {}

        def members(r):
            return range(r * GROUP, (r + 1) * GROUP)

        def rotated(r):
            return 0 <= r < groups and units[r // UNIT_ROUNDS][2] is not None

        def plain(r):
            return 0 <= r < groups and units[r // UNIT_ROUNDS][2] is None

        def load_chunk(j):
            n, g = divmod(j, PASSES)
            weight, first_col = units[n][0], units[n][3]
            raw = raw_pool.tile([P, PACK, UNIT_COLS], BF16, name="raw")
            nc.sync.dma_start(
                out=raw[:],
                in_=weight[g * K_PASS : (g + 1) * K_PASS, first_col : first_col + UNIT_COLS].rearrange(
                    "(p t) c -> p t c", t=PACK
                ),
            )
            raw_of[j] = raw

        def regroup(j):
            raw = raw_of[j]
            grouped = grouped_pool.tile([P, UNIT_COLS, PACK], BF16, align_bytes=64, name="grouped")
            r = j // GROUP - REGROUP_AHEAD
            vector_cols = VECTOR_COLS[(rotated(r - SQUARES_AFTER), rotated(r - PRODUCTS_AFTER))]
            if j < PASSES:
                vector_cols = FIRST_UNIT_VECTOR_COLS
            nc.vector.tensor_copy(
                out=grouped[:, :vector_cols, :].rearrange("p (c i) t -> p c t i", i=RUN),
                in_=raw[:, :, :vector_cols].rearrange("p t (c i) -> p c t i", i=RUN),
            )
            nc.scalar.copy(
                out=grouped[:, vector_cols:, :].rearrange("p (c i) t -> p c t i", i=RUN),
                in_=raw[:, :, vector_cols:].rearrange("p t (c i) -> p c t i", i=RUN),
            )
            grouped_of[j] = grouped
            if j + RAW_CHUNKS < chunks:
                load_chunk(j + RAW_CHUNKS)

        def quantise(j):
            w_words = packed_pool.tile([P, UNIT_COLS], U32, align_bytes=64, name="w_words")
            w_scales = packed_pool.tile([P, UNIT_COLS], U8, align_bytes=64, name="w_scales")
            nc.vector.quantize_mx(
                out=w_words[:].bitcast(FP8X4),
                scales=w_scales[:],
                in_=grouped_of[j][:].rearrange("p c t -> p (c t)"),
            )
            packed_of[j] = (w_words, w_scales)

        def multiply(j):
            n, g = divmod(j, PASSES)
            w_words, w_scales = packed_of[j]
            for m in range(TILES):
                b = n * TILES + m
                if g == 0:
                    bank_of[b] = psum.tile([P, UNIT_COLS], F32, name="bank", tag="bank")
                nc.tensor.matmul_mx(
                    out=bank_of[b][:],
                    lhsT=x_words[:, m, g, :].bitcast(FP8X4),
                    lhsT_scale=x_scales[:, m, g, :],
                    rhs=w_words[:].bitcast(FP8X4),
                    rhs_scale=w_scales[:],
                    start=(g == 0),
                    stop=(g == PASSES - 1),
                )

        def turn_and_quantise_positions(m):
            x_grouped = x_stage.tile([P, PASSES, P, PACK], BF16, align_bytes=64, name="x_grouped")
            x_grouped_f32 = x_grouped[:].bitcast(F32)
            words = x_tiles[m][:].bitcast(F32).rearrange("s (g p u) -> s g u p", g=PASSES, u=PAIRS)
            for first_pass, copy in ((0, nc.scalar.copy), (2, nc.vector.tensor_copy)):
                turned = psum.tile([P, 2, PAIRS, P], F32, name="turned", tag="bank")
                for i in range(2):
                    for u in range(PAIRS):
                        nc.tensor.transpose(turned[:, i, u, :], words[:, first_pass + i, u, :], identity[:])
                copy(
                    out=x_grouped_f32[:, first_pass : first_pass + 2, :, :],
                    in_=turned[:].rearrange("p g u s -> p g s u"),
                )
            nc.vector.quantize_mx(
                out=x_words[:, m, :, :].rearrange("p g s -> p (g s)").bitcast(FP8X4),
                scales=x_scales[:, m, :, :].rearrange("p g s -> p (g s)"),
                in_=x_grouped[:].rearrange("p g s t -> p (g s t)"),
            )

        def build_tables(tables_name, gain_sb):
            table = const.tile([P, TILES, 2, HEAD_DIM], F32, name="table_" + tables_name)
            for j, half, trig in ((0, low, cos_sb), (1, low, sin_sb), (1, high, cos_sb)):
                source = low if j == 0 else high
                nc.vector.tensor_tensor(
                    out=table[:, :, j, half],
                    in0=trig[:, :, source],
                    in1=gain_sb[:, half].unsqueeze(1).to_broadcast([P, TILES, HALF]),
                    op=ALU.mult,
                )
            nc.vector.scalar_tensor_tensor(
                out=table[:, :, 0, high],
                in0=sin_sb[:, :, low],
                scalar=-1.0,
                in1=gain_sb[:, high].unsqueeze(1).to_broadcast([P, TILES, HALF]),
                op0=ALU.mult,
                op1=ALU.mult,
            )
            tables[tables_name] = table

        def store(b):
            n, m = divmod(b, TILES)
            rows, first_col = units[n][1], units[n][3]
            nc.sync.dma_start(
                out=rows[m * P : (m + 1) * P, first_col : first_col + UNIT_COLS],
                in_=result_of[b // GROUP][:, b % GROUP, :, :].rearrange("p h d -> p (h d)"),
            )

        def sum_squares(r):
            square_sums = scratch_pool.tile([P, GROUP * UNIT_HEADS], F32, name="square_sums")
            rinv = scratch_pool.tile([P, GROUP * UNIT_HEADS], F32, name="rinv")
            norm_of[r] = (square_sums, rinv)
            for i, b in enumerate(members(r)):
                squares = scratch_pool.tile([P, UNIT_COLS], BF16, name="squares")
                for h in range(UNIT_HEADS):
                    head = slice(h * HEAD_DIM, (h + 1) * HEAD_DIM)
                    column = i * UNIT_HEADS + h
                    nc.scalar.activation(
                        out=squares[:, head],
                        in_=bank_of[b][:, head],
                        func=ACT.Square,
                        accum_out=square_sums[:, column : column + 1],
                    )

        def invert_rms(r):
            square_sums, rinv = norm_of[r]
            nc.scalar.activation(
                out=rinv[:],
                in_=square_sums[:],
                func=ACT.Abs_reciprocal_sqrt,
                scale=1.0 / HEAD_DIM,
                bias=eps_column[:],
            )

        def rotary_products(r):
            rinv = norm_of[r][1]
            result = result_pool.tile([P, GROUP, UNIT_HEADS, HEAD_DIM], F32, name="result")
            products = scratch_pool.tile([P, GROUP, UNIT_HEADS, 2, HEAD_DIM], F32, name="products")
            for i, b in enumerate(members(r)):
                n, m = divmod(b, TILES)
                u = bank_of[b][:].rearrange("p (h d) -> p h d", d=HEAD_DIM)
                for h in range(UNIT_HEADS):
                    column = i * UNIT_HEADS + h
                    nc.vector.scalar_tensor_tensor(
                        out=products[:, i, h, :, :],
                        in0=u[:, h, :].unsqueeze(1).to_broadcast([P, 2, HEAD_DIM]),
                        scalar=rinv[:, column : column + 1],
                        in1=tables[units[n][2]][:, m, :, :],
                        op0=ALU.mult,
                        op1=ALU.mult,
                    )
            result_of[r] = result
            halves = products[:].rearrange("p i h j (two e) -> p (i h j) two e", two=2)
            nc.gpsimd.tensor_tensor(
                out=result[:].rearrange("p i h (j e) -> p (i h j) e", j=2),
                in0=halves[:, :, 0, :],
                in1=halves[:, :, 1, :],
                op=ALU.add,
            )

        def copy_out_and_store(r):
            result = result_pool.tile([P, GROUP, UNIT_HEADS, HEAD_DIM], F32, name="result")
            result_of[r] = result
            for i, b in enumerate(members(r)):
                copy = nc.scalar.copy if b % 2 == 0 else nc.vector.tensor_copy
                copy(out=result[:, i, :, :].rearrange("p h d -> p (h d)"), in_=bank_of[b][:])
                store(b)

        def do_round(r):
            if rotated(r - PRODUCTS_AFTER):
                invert_rms(r - PRODUCTS_AFTER)
            if r + REGROUP_AHEAD < groups:
                for j in members(r + REGROUP_AHEAD):
                    regroup(j)
            if UNIT_ROUNDS <= r < groups:
                for j in members(r):
                    quantise(j)
            if rotated(r - PRODUCTS_AFTER):
                rotary_products(r - PRODUCTS_AFTER)
            if UNIT_ROUNDS <= r < groups:
                for j in members(r):
                    multiply(j)
            if plain(r - PRODUCTS_AFTER):
                copy_out_and_store(r - PRODUCTS_AFTER)
            if rotated(r - SQUARES_AFTER):
                sum_squares(r - SQUARES_AFTER)
            if rotated(r - STORE_AFTER):
                for b in members(r - STORE_AFTER):
                    store(b)

        x_tiles = []
        for m in range(TILES):
            load_chunk(m)
            x_tile = const.tile([P, MODEL_DIM], BF16, name="x_tile%d" % m)
            nc.sync.dma_start(out=x_tile[:], in_=x_rows[m * P : (m + 1) * P, :])
            x_tiles.append(x_tile)
        for j in range(PASSES, 2 * PASSES):
            load_chunk(j)
        cos_sb = const.tile([P, TILES, HEAD_DIM], BF16)
        nc.sync.dma_start(out=cos_sb[:], in_=cos.rearrange("b s d -> (b s) d").rearrange("(m p) d -> p m d", p=P))
        sin_sb = const.tile([P, TILES, HEAD_DIM], BF16)
        nc.sync.dma_start(out=sin_sb[:], in_=sin.rearrange("b s d -> (b s) d").rearrange("(m p) d -> p m d", p=P))
        q_gain = const.tile([P, HEAD_DIM], BF16)
        nc.sync.dma_start(out=q_gain[:], in_=q_scale.partition_broadcast(P))
        k_gain = const.tile([P, HEAD_DIM], BF16)
        nc.sync.dma_start(out=k_gain[:], in_=k_scale.partition_broadcast(P))
        for j in range(2 * PASSES, RAW_CHUNKS):
            load_chunk(j)

        identity = const.tile([P, P], F32)
        make_identity(nc, identity[:])
        eps_column = const.tile([P, 1], F32)
        nc.vector.memset(eps_column[:], EPS)
        warm_up = const.tile([P, 1], F32)
        nc.scalar.activation(out=warm_up[:], in_=eps_column[:], func=ACT.Abs_reciprocal_sqrt)
        x_words = const.tile([P, TILES, PASSES, P], U32, align_bytes=64)
        x_scales = const.tile([P, TILES, PASSES, P], U8, align_bytes=64)

        for j in range(PASSES):
            regroup(j)
            if j > 0:
                turn_and_quantise_positions(j - 1)
            quantise(j)
        turn_and_quantise_positions(TILES - 1)
        for j in range(PASSES):
            multiply(j)
        for r in range(UNIT_ROUNDS - REGROUP_AHEAD, PRODUCTS_AFTER):
            do_round(r)
        build_tables("q", q_gain)
        build_tables("k", k_gain)
        for r in range(PRODUCTS_AFTER, groups + PRODUCTS_AFTER):
            do_round(r)
